import numpy as np
import ml_dtypes


def mxq(x, axis, fmt="e4m3"):
    dtype, down = {"e4m3": (ml_dtypes.float8_e4m3fn, 7), "e5m2": (ml_dtypes.float8_e5m2, 14)}[fmt]
    v = np.moveaxis(np.asarray(x, np.float32).astype(ml_dtypes.bfloat16).astype(np.float64), axis, -1)
    blocks = v.reshape(v.shape[:-1] + (-1, 32))
    amax = np.abs(blocks).max(-1, keepdims=True)
    byte = np.maximum(np.where(amax > 0, np.frexp(amax)[1] - 1 + 127, 0) - down, 1)
    scale = np.exp2(byte - 127.0)
    codes = (blocks / scale).astype(np.float32).astype(dtype).astype(np.float64)
    return np.moveaxis((codes * scale).reshape(v.shape), -1, axis)


WIDE = False


def mx_kscale(k):
    if not WIDE:
        return np.ones(k)
    levels = np.array([10, -10, 5, -5, 0])
    if k % 512:
        return np.exp2(np.random.permutation(np.resize(levels, k // 32))).repeat(32)
    a = np.empty((k // 512, 16))
    for p in range(k // 512):
        a[p, :8] = np.random.permutation(np.resize(levels, 8))
        for g in range(8):
            far = levels[np.abs(levels - a[p, g]) >= 10]
            a[p, g + 8] = far[np.random.randint(len(far))]
    return np.exp2(a.ravel()).repeat(32)


BF16 = ml_dtypes.bfloat16


def bf(x):
    return np.asarray(x, np.float32).astype(BF16)


def f64(x):
    return np.asarray(x).astype(np.float64)


B, T, E = 32, 256, 512


def setup_inputs():
    s, t = mx_kscale(E), mx_kscale(E)
    r = np.random.standard_normal
    return {"x1": bf(r((B, T, E)) * s), "x2": bf(r((B, T, E)) * s),
            "W1": bf(r((E, E)) * 0.4 / np.sqrt(E) / s[:, None] * t), "W2": bf(r((E, E)) * 0.4 / np.sqrt(E) / s[:, None] / t),
            "b1": bf(r((T, E)) * 0.1 * t), "b2": bf(r((T, E)) * 0.1 / t)}


def reference(x1, x2, W1, W2, b1, b2):
    e1t = np.maximum((mxq(f64(x1), 2, "e4m3") @ mxq(f64(W1), 0, "e4m3")) + f64(b1), 0.0)
    e2t = np.maximum((mxq(f64(x2), 2, "e4m3") @ mxq(f64(W2), 0, "e4m3")) + f64(b2), 0.0)
    scores = mxq(e2t, 2, "e4m3") @ mxq(e1t, 2, "e4m3").transpose(0, 2, 1)
    ex = np.exp(scores - scores.max(-1, keepdims=True))
    return ex / ex.sum(-1, keepdims=True)

@@ -1,0 +1,440 @@
+from contextlib import ExitStack
+
+import concourse.mybir as mybir
+from concourse.masks import make_identity
+
+FLOPS = 2 * (2 * 8192 * 512 * 512) + 2 * 32 * 256 * 256 * 512
+
+BF16 = mybir.dt.bfloat16
+F32 = mybir.dt.float32
+U32 = mybir.dt.uint32
+U8 = mybir.dt.uint8
+FP8X4 = mybir.dt.float8_e4m3fn_x4
+ALU = mybir.AluOpType
+ACT = mybir.ActivationFunctionType
+
+P = 128
+B, T, E = 32, 256, 512
+UNIT = 512
+N_UNITS = B * T // UNIT
+LOAD_AHEAD = 6
+BIG = 3.4028234e38
+
+
+def tile_attentionmm_pa_t_kernel(tc, x1, x2, W1, W2, b1, b2, out):
+    nc = tc.nc
+    xs_dram = [x1.rearrange("b t k -> (b t) k"), x2.rearrange("b t k -> (b t) k")]
+    ws_dram = [W1, W2]
+    bs_dram = [b1, b2]
+    out_view = out.rearrange("b (c p) j -> p (b c) j", p=P)
+
+    with ExitStack() as ctx:
+        ctx.enter_context(tc.manual_schedule())
+        const = ctx.enter_context(tc.tile_pool(name="const", bufs=1))
+        xin = ctx.enter_context(tc.tile_pool(name="xin", bufs=2 * LOAD_AHEAD))
+        work = ctx.enter_context(tc.tile_pool(name="work", bufs=3))
+        small = ctx.enter_context(tc.tile_pool(name="small", bufs=4))
+        psum = ctx.enter_context(tc.psum_pool(name="psum", bufs=2))
+
+        live = {}
+        w_raw, b_raw, w_grp, w_codes, w_scales, bias_t = [], [], [], [], [], []
+
+        def ok(i):
+            return 0 <= i < N_UNITS
+
+        def load_x(i, s):
+            if not ok(i):
+                return
+            x_sb = xin.tile([P, 4 * E], BF16, name="x_sb", tag="x_sb")
+            nc.sync.dma_start(
+                out=x_sb[:].rearrange("p (n k) -> p n k", n=4),
+                in_=xs_dram[s][i * UNIT : (i + 1) * UNIT, :].rearrange("(n p) k -> p n k", p=P),
+            )
+            live[("x", i, s)] = x_sb
+
+        def load_w(s):
+            wr = const.tile([P, 4 * E], BF16, name="w_raw%d" % s)
+            nc.sync.dma_start(
+                out=wr[:],
+                in_=ws_dram[s].rearrange("(p j) f -> p (j f)", j=4),
+            )
+            w_raw.append(wr)
+
+        def load_b(s):
+            br = const.tile([P, 2 * E], BF16, name="b_raw%d" % s)
+            nc.sync.dma_start(
+                out=br[:].rearrange("p (h f) -> p h f", h=2),
+                in_=bs_dram[s].rearrange("(h p) f -> p h f", p=P),
+            )
+            b_raw.append(br)
+
+        def regroup_w(s, on_vector):
+            wg = const.tile([P, 4 * E], BF16, name="w_grp%d" % s, align_bytes=64)
+            dst = wg[:].rearrange("p (c m j) -> p c m j", c=4, j=4)
+            src = w_raw[s][:].rearrange("p (j m c) -> p c m j", j=4, c=4)
+            if on_vector:
+                nc.vector.tensor_copy(out=dst, in_=src)
+            else:
+                nc.gpsimd.tensor_scalar(
+                    out=dst, in0=src, scalar1=1.0, scalar2=0.0, op0=ALU.mult, op1=ALU.add
+                )
+            w_grp.append(wg)
+
+        def quantise_w(s):
+            wc = const.tile([P, E], U32, name="w_codes%d" % s, align_bytes=64)
+            wsc = const.tile([P, E], U8, name="w_scales%d" % s, align_bytes=64)
+            nc.vector.quantize_mx(out=wc[:].bitcast(FP8X4), scales=wsc[:], in_=w_grp[s][:])
+            w_codes.append(wc)
+            w_scales.append(wsc)
+
+        def transpose_b(s):
+            bt = psum.tile([P, 8 * P], BF16, name="bt", tag="sc")
+            for h in range(2):
+                for c in range(4):
+                    nc.tensor.transpose(
+                        bt[:, (h * 4 + c) * P : (h * 4 + c + 1) * P],
+                        b_raw[s][:, h * E + c : (h + 1) * E : 4],
+                        ident_bf[:],
+                    )
+            live[("bt", s)] = bt
+
+        def drain_b(s):
+            bias = const.tile([P, T * 4], BF16, name="bias_t%d" % s)
+            nc.scalar.copy(
+                out=bias[:].rearrange("p (h t c) -> p h t c", h=2, c=4),
+                in_=live[("bt", s)][:].rearrange("p (h c t) -> p h t c", h=2, c=4),
+            )
+            bias_t.append(bias)
+            if s == 1:
+                plain = const.tile([P, 8 * P], BF16, name="bias_plain")
+                nc.scalar.copy(out=plain[:], in_=live[("bt", s)][:])
+                live["bias_plain"] = plain
+
+        def transpose_x(i, s):
+            if not ok(i):
+                return
+            x_f32 = live[("x", i, s)][:].bitcast(F32)
+            for h in range(2):
+                xt = psum.tile([P, 512], F32, name="xt", tag="xt")
+                for nn in range(2):
+                    for u in range(2):
+                        n = 2 * h + nn
+                        nc.tensor.transpose(
+                            xt[:, u * 256 + nn * P : u * 256 + (nn + 1) * P],
+                            x_f32[:, n * 256 + u : (n + 1) * 256 : 2],
+                            ident[:],
+                        )
+                live[("xt", i, s, h)] = xt
+
+        def drain_x(i, s):
+            if not ok(i):
+                return
+            xg = work.tile([P, 4 * UNIT], BF16, name="xg", tag="xg", align_bytes=64)
+            xg_f32 = xg[:].bitcast(F32)
+            for h in range(2):
+                nc.scalar.copy(
+                    out=xg_f32[:, h * 512 : (h + 1) * 512].rearrange("p (t u) -> p t u", u=2),
+                    in_=live[("xt", i, s, h)][:].rearrange("p (u t) -> p t u", u=2),
+                )
+            live[("xg", i, s)] = xg
+
+        def quantise_x(i, s):
+            if not ok(i):
+                return
+            xc = work.tile([P, UNIT], U32, name="xc", tag="xc", align_bytes=64)
+            xsc = work.tile([P, UNIT], U8, name="xsc", tag="xsc", align_bytes=64)
+            nc.vector.quantize_mx(out=xc[:].bitcast(FP8X4), scales=xsc[:], in_=live[("xg", i, s)][:])
+            live[("xc", i, s)] = (xc, xsc)
+
+        def project(i, s, n):
+            if not ok(i):
+                return
+            xc, xsc = live[("xc", i, s)]
+            s1 = psum.tile([P, 512], F32, name="s1", tag="s1", bufs=4)
+            for c in range(4):
+                nc.tensor.matmul_mx(
+                    out=s1[:, c * P : (c + 1) * P],
+                    lhsT=w_codes[s][:, c * P : (c + 1) * P].bitcast(FP8X4),
+                    lhsT_scale=w_scales[s][:, c * P : (c + 1) * P],
+                    rhs=xc[:, n * P : (n + 1) * P].bitcast(FP8X4),
+                    rhs_scale=xsc[:, n * P : (n + 1) * P],
+                    start=True,
+                    stop=True,
+                )
+            live[("s1", i, s, n)] = s1
+
+        def add_bias(i, s, n):
+            if not ok(i):
+                return
+            if n == 0:
+                live[("eg", i, s)] = work.tile(
+                    [P, 4 * UNIT], BF16, name="eg", tag="eg", align_bytes=64
+                )
+            eg = live[("eg", i, s)]
+            t0 = (n % 2) * P
+            nc.vector.tensor_tensor(
+                out=eg[:, n * 512 : (n + 1) * 512].rearrange("p (t c) -> p t c", c=4),
+                in0=live[("s1", i, s, n)][:].rearrange("p (c t) -> p t c", c=4),
+                in1=bias_t[s][:, t0 * 4 : (t0 + P) * 4].rearrange("p (t c) -> p t c", c=4),
+                op=ALU.add,
+            )
+
+        def relu_pool(i, s, lo, hi):
+            if not ok(i):
+                return
+            eg = live[("eg", i, s)]
+            nc.gpsimd.tensor_scalar(
+                out=eg[:, lo:hi], in0=eg[:, lo:hi], scalar1=BIG, scalar2=0.0, op0=ALU.min, op1=ALU.max
+            )
+
+        def relu_act(i, s, lo, hi):
+            if not ok(i):
+                return
+            eg = live[("eg", i, s)]
+            nc.scalar.activation(out=eg[:, lo:hi], in_=eg[:, lo:hi], func=ACT.Relu)
+
+        def relu_vec(i, s, lo, hi):
+            eg = live[("eg", i, s)]
+            nc.vector.tensor_scalar_max(out=eg[:, lo:hi], in0=eg[:, lo:hi], scalar1=0.0)
+
+        def quantise_e(i, s, lo, hi):
+            if not ok(i):
+                return
+            if lo == 0:
+                ec = work.tile([P, UNIT], U32, name="ec", tag="ec", bufs=4, align_bytes=64)
+                esc = work.tile([P, UNIT], U8, name="esc", tag="esc", bufs=4, align_bytes=64)
+                live[("ec", i, s)] = (ec, esc)
+            ec, esc = live[("ec", i, s)]
+            nc.vector.quantize_mx(
+                out=ec[:, lo // 4 : hi // 4].bitcast(FP8X4),
+                scales=esc[:, lo // 4 : hi // 4],
+                in_=live[("eg", i, s)][:, lo:hi],
+            )
+
+        def scores(i, bb):
+            if not ok(i):
+                return
+            e1c, e1s = live[("ec", i, 0)]
+            e2c, e2s = live[("ec", i, 1)]
+            sc = psum.tile([P, 512], F32, name="sc", tag="sc")
+            for c in range(2):
+                nc.tensor.matmul_mx(
+                    out=sc[:, c * T : (c + 1) * T],
+                    lhsT=e2c[:, bb * T + c * P : bb * T + (c + 1) * P].bitcast(FP8X4),
+                    lhsT_scale=e2s[:, bb * T + c * P : bb * T + (c + 1) * P],
+                    rhs=e1c[:, bb * T : (bb + 1) * T].bitcast(FP8X4),
+                    rhs_scale=e1s[:, bb * T : (bb + 1) * T],
+                    start=True,
+                    stop=True,
+                )
+            live[("sc", i, bb)] = sc
+
+        def row_max(i, bb, c0, c1):
+            if not ok(i):
+                return
+            if bb == 0 and c0 == 0:
+                live[("neg_max", i)] = small.tile([P, 4], F32, name="neg_max", tag="neg_max")
+                live[("sums", i)] = small.tile([P, 4], F32, name="sums", tag="sums")
+                live[("ex", i)] = work.tile([P, 4 * T], F32, name="ex", tag="ex", bufs=4)
+            nc.vector.tensor_reduce(
+                out=live[("neg_max", i)][:, 2 * bb + c0 : 2 * bb + c1],
+                in_=live[("sc", i, bb)][:, c0 * T : c1 * T].rearrange("p (c j) -> p c j", j=T),
+                axis=mybir.AxisListType.X,
+                op=ALU.max,
+                negate=True,
+            )
+
+        def exps(i, bb, c):
+            if not ok(i):
+                return
+            q = 2 * bb + c
+            nc.scalar.activation(
+                out=live[("ex", i)][:, q * T : (q + 1) * T],
+                in_=live[("sc", i, bb)][:, c * T : (c + 1) * T],
+                func=ACT.Exp,
+                bias=live[("neg_max", i)][:, q : q + 1],
+                scale=1.0,
+                accum_out=live[("sums", i)][:, q : q + 1],
+            )
+
+        def reciprocals(i, q0, q1):
+            if not ok(i):
+                return
+            if q0 == 0:
+                live[("recip", i)] = small.tile([P, 4], F32, name="recip", tag="recip")
+            nc.vector.reciprocal(out=live[("recip", i)][:, q0:q1], in_=live[("sums", i)][:, q0:q1])
+
+        def scale_pool(i, q):
+            if not ok(i):
+                return
+            ex = live[("ex", i)]
+            nc.gpsimd.tensor_scalar(
+                out=ex[:, q * T : (q + 1) * T],
+                in0=ex[:, q * T : (q + 1) * T],
+                scalar1=live[("recip", i)][:, q : q + 1],
+                scalar2=0.0,
+                op0=ALU.mult,
+                op1=ALU.add,
+            )
+
+        def scale_vec(i, q):
+            ex = live[("ex", i)]
+            nc.vector.tensor_scalar_mul(
+                out=ex[:, q * T : (q + 1) * T],
+                in0=ex[:, q * T : (q + 1) * T],
+                scalar1=live[("recip", i)][:, q : q + 1],
+            )
+
+        def store(i, q0, q1):
+            if not ok(i):
+                return
+            nc.sync.dma_start(
+                out=out_view[:, 4 * i + q0 : 4 * i + q1, :],
+                in_=live[("ex", i)][:, q0 * T : q1 * T].rearrange("p (q j) -> p q j", j=T),
+            )
+
+        def max_and_exp(i):
+            for bb in range(2):
+                row_max(i, bb, 0, 2)
+                exps(i, bb, 0)
+                exps(i, bb, 1)
+
+        def normalise(i, q0, q1):
+            reciprocals(i, q0, q1)
+            for q in range(q0, q1):
+                scale_pool(i, q)
+
+        def detour_out(i):
+            a_sb = work.tile([P, 512], F32, name="a_sb", tag="a_sb")
+            nc.scalar.copy(out=a_sb[:], in_=live[("s1", i, 1, 3)][:])
+            live[("a_sb", i)] = a_sb
+
+        def detour_add(i):
+            pb = psum.tile([P, 512], F32, name="pb", tag="s1", bufs=4)
+            nc.tensor.matmul(pb[:], lhsT=ident[:], rhs=live[("a_sb", i)][:], start=True, stop=False)
+            nc.tensor.matmul(
+                pb[:], lhsT=ident_bf[:], rhs=live["bias_plain"][:, 512:1024], start=False, stop=True
+            )
+            live[("pb", i)] = pb
+
+        def detour_relu(i):
+            nc.scalar.activation(
+                out=live[("eg", i, 1)][:, 1536:2048].rearrange("p (t c) -> p t c", c=4),
+                in_=live[("pb", i)][:].rearrange("p (c t) -> p t c", c=4),
+                func=ACT.Relu,
+            )
+
+        def first_half(i):
+            load_x(i + LOAD_AHEAD, 0)
+            load_x(i + LOAD_AHEAD, 1)
+            drain_x(i + 1, 0)
+            for n in range(4):
+                add_bias(i, 0, n)
+                if n == 0:
+                    relu_pool(i, 0, 0, 512)
+                if i > 0:
+                    project(i, 1, n)
+            if i == 0:
+                quantise_w(1)
+                quantise_x(0, 1)
+                for n in range(4):
+                    project(0, 1, n)
+            relu_act(i, 0, 1024, 2048)
+            relu_vec(i, 0, 512, 1024)
+            if i < N_UNITS - 1:
+                detour_out(i)
+            transpose_x(i + 1, 1)
+            quantise_e(i - 1, 1, 0, 4 * UNIT)
+            scores(i - 1, 0)
+            scores(i - 1, 1)
+            quantise_x(i + 1, 0)
+
+        def second_half(i):
+            drain_x(i + 1, 1)
+            normalise(i - 3, 3, 4)
+            store(i - 3, 0, 4)
+            add_bias(i, 1, 0)
+            relu_pool(i, 1, 0, 512)
+            detour_add(i)
+            add_bias(i, 1, 1)
+            project(i + 1, 0, 0)
+            add_bias(i, 1, 2)
+            project(i + 1, 0, 1)
+            project(i + 1, 0, 2)
+            relu_act(i, 1, 512, 1536)
+            detour_relu(i)
+            project(i + 1, 0, 3)
+            transpose_x(i + 2, 0)
+            quantise_e(i, 0, 0, 4 * UNIT)
+            quantise_x(i + 1, 1)
+            normalise(i - 2, 0, 3)
+            max_and_exp(i - 1)
+
+        def tail(i):
+            half = 2 * UNIT
+            normalise(i - 3, 3, 4)
+            store(i - 3, 0, 4)
+            add_bias(i, 1, 0)
+            add_bias(i, 1, 1)
+            normalise(i - 2, 0, 4)
+            store(i - 2, 0, 4)
+            max_and_exp(i - 1)
+            relu_vec(i, 1, 0, half)
+            quantise_e(i, 0, 0, 4 * UNIT)
+            add_bias(i, 1, 2)
+            quantise_e(i, 1, 0, half)
+            scores(i, 0)
+            add_bias(i, 1, 3)
+            normalise(i - 1, 0, 4)
+            store(i - 1, 0, 4)
+            relu_vec(i, 1, half, 2 * half)
+            row_max(i, 0, 0, 2)
+            exps(i, 0, 0)
+            exps(i, 0, 1)
+            quantise_e(i, 1, half, 2 * half)
+            scores(i, 1)
+            row_max(i, 1, 0, 1)
+            exps(i, 1, 0)
+            row_max(i, 1, 1, 2)
+            exps(i, 1, 1)
+            for bb in range(2):
+                reciprocals(i, 2 * bb, 2 * bb + 2)
+                scale_vec(i, 2 * bb)
+                scale_vec(i, 2 * bb + 1)
+                store(i, 2 * bb, 2 * bb + 2)
+
+        ident = const.tile([P, P], F32, name="ident")
+        make_identity(nc, ident[:])
+        ident_bf = const.tile([P, P], BF16, name="ident_bf")
+        make_identity(nc, ident_bf[:])
+        load_w(0)
+        load_x(0, 0)
+        load_w(1)
+        load_b(0)
+        load_x(0, 1)
+        load_b(1)
+        for i in range(1, LOAD_AHEAD):
+            load_x(i, 0)
+            load_x(i, 1)
+
+        regroup_w(0, True)
+        regroup_w(1, False)
+        transpose_x(0, 0)
+        drain_x(0, 0)
+        quantise_w(0)
+        transpose_b(0)
+        drain_b(0)
+        quantise_x(0, 0)
+        for n in range(4):
+            project(0, 0, n)
+        transpose_x(0, 1)
+        drain_x(0, 1)
+        transpose_b(1)
+        drain_b(1)
+        transpose_x(1, 0)
+
+        for i in range(N_UNITS - 1):
+            first_half(i)
+            second_half(i)
+        first_half(N_UNITS - 1)
+        tail(N_UNITS - 1)

@@ -42,15 +42,15 @@ def tile_attentionmm_pa_t_kernel(tc, x1, x2, W1, W2, b1, b2, out):
         def ok(i):
             return 0 <= i < N_UNITS
 
-        def load_x(i, s):
+        def load_x(i, s, n0=0, n1=4):
             if not ok(i):
                 return
-            x_sb = xin.tile([P, 4 * E], BF16, name="x_sb", tag="x_sb")
+            if n0 == 0:
+                live[("x", i, s)] = xin.tile([P, 4 * E], BF16, name="x_sb", tag="x_sb")
             nc.sync.dma_start(
-                out=x_sb[:].rearrange("p (n k) -> p n k", n=4),
-                in_=xs_dram[s][i * UNIT : (i + 1) * UNIT, :].rearrange("(n p) k -> p n k", p=P),
+                out=live[("x", i, s)][:, n0 * E : n1 * E].rearrange("p (n k) -> p n k", n=n1 - n0),
+                in_=xs_dram[s][i * UNIT + n0 * P : i * UNIT + n1 * P, :].rearrange("(n p) k -> p n k", p=P),
             )
-            live[("x", i, s)] = x_sb
 
         def load_w(s):
             wr = const.tile([P, 4 * E], BF16, name="w_raw%d" % s)
@@ -68,16 +68,11 @@ def tile_attentionmm_pa_t_kernel(tc, x1, x2, W1, W2, b1, b2, out):
             )
             b_raw.append(br)
 
-        def regroup_w(s, on_vector):
+        def regroup_w(s):
             wg = const.tile([P, 4 * E], BF16, name="w_grp%d" % s, align_bytes=64)
             dst = wg[:].rearrange("p (c m j) -> p c m j", c=4, j=4)
             src = w_raw[s][:].rearrange("p (j m c) -> p c m j", j=4, c=4)
-            if on_vector:
-                nc.vector.tensor_copy(out=dst, in_=src)
-            else:
-                nc.gpsimd.tensor_scalar(
-                    out=dst, in0=src, scalar1=1.0, scalar2=0.0, op0=ALU.mult, op1=ALU.add
-                )
+            nc.vector.tensor_copy(out=dst, in_=src)
             w_grp.append(wg)
 
         def quantise_w(s):
@@ -88,33 +83,33 @@ def tile_attentionmm_pa_t_kernel(tc, x1, x2, W1, W2, b1, b2, out):
             w_scales.append(wsc)
 
         def transpose_b(s):
-            bt = psum.tile([P, 8 * P], BF16, name="bt", tag="sc")
+            bias_t.append(const.tile([P, T * 4], BF16, name="bias_t%d" % s))
             for h in range(2):
+                bt = psum.tile([P, 4 * P], BF16, name="bt", tag="sc")
                 for c in range(4):
                     nc.tensor.transpose(
-                        bt[:, (h * 4 + c) * P : (h * 4 + c + 1) * P],
+                        bt[:, c * P : (c + 1) * P],
                         b_raw[s][:, h * E + c : (h + 1) * E : 4],
                         ident_bf[:],
                     )
-            live[("bt", s)] = bt
+                live[("bt", s, h)] = bt
 
-        def drain_b(s):
-            bias = const.tile([P, T * 4], BF16, name="bias_t%d" % s)
+        def drain_b(s, h):
+            bt = live[("bt", s, h)]
             nc.scalar.copy(
-                out=bias[:].rearrange("p (h t c) -> p h t c", h=2, c=4),
-                in_=live[("bt", s)][:].rearrange("p (h c t) -> p h t c", h=2, c=4),
+                out=bias_t[s][:, h * 512 : (h + 1) * 512].rearrange("p (t c) -> p t c", c=4),
+                in_=bt[:].rearrange("p (c t) -> p t c", c=4),
             )
-            bias_t.append(bias)
-            if s == 1:
-                plain = const.tile([P, 8 * P], BF16, name="bias_plain")
-                nc.scalar.copy(out=plain[:], in_=live[("bt", s)][:])
+            if s == 1 and h == 1:
+                plain = const.tile([P, 4 * P], BF16, name="bias_plain")
+                nc.scalar.copy(out=plain[:], in_=bt[:])
                 live["bias_plain"] = plain
 
-        def transpose_x(i, s):
+        def transpose_x(i, s, halves=(0, 1)):
             if not ok(i):
                 return
             x_f32 = live[("x", i, s)][:].bitcast(F32)
-            for h in range(2):
+            for h in halves:
                 xt = psum.tile([P, 512], F32, name="xt", tag="xt")
                 for nn in range(2):
                     for u in range(2):
@@ -126,31 +121,39 @@ def tile_attentionmm_pa_t_kernel(tc, x1, x2, W1, W2, b1, b2, out):
                         )
                 live[("xt", i, s, h)] = xt
 
-        def drain_x(i, s):
+        def drain_x(i, s, halves=(0, 1)):
             if not ok(i):
                 return
-            xg = work.tile([P, 4 * UNIT], BF16, name="xg", tag="xg", align_bytes=64)
-            xg_f32 = xg[:].bitcast(F32)
-            for h in range(2):
+            if halves[0] == 0:
+                live[("xg", i, s)] = work.tile([P, 4 * UNIT], BF16, name="xg", tag="xg", align_bytes=64)
+            xg_f32 = live[("xg", i, s)][:].bitcast(F32)
+            for h in halves:
                 nc.scalar.copy(
                     out=xg_f32[:, h * 512 : (h + 1) * 512].rearrange("p (t u) -> p t u", u=2),
                     in_=live[("xt", i, s, h)][:].rearrange("p (u t) -> p t u", u=2),
                 )
-            live[("xg", i, s)] = xg
 
-        def quantise_x(i, s):
+        def quantise_x(i, s, lo=0, hi=4 * UNIT):
             if not ok(i):
                 return
-            xc = work.tile([P, UNIT], U32, name="xc", tag="xc", align_bytes=64)
-            xsc = work.tile([P, UNIT], U8, name="xsc", tag="xsc", align_bytes=64)
-            nc.vector.quantize_mx(out=xc[:].bitcast(FP8X4), scales=xsc[:], in_=live[("xg", i, s)][:])
-            live[("xc", i, s)] = (xc, xsc)
+            if lo == 0:
+                xc = work.tile([P, UNIT], U32, name="xc", tag="xc", align_bytes=64)
+                xsc = work.tile([P, UNIT], U8, name="xsc", tag="xsc", align_bytes=64)
+                live[("xc", i, s)] = (xc, xsc)
+            xc, xsc = live[("xc", i, s)]
+            nc.vector.quantize_mx(
+                out=xc[:, lo // 4 : hi // 4].bitcast(FP8X4),
+                scales=xsc[:, lo // 4 : hi // 4],
+                in_=live[("xg", i, s)][:, lo:hi],
+            )
 
-        def project(i, s, n):
+        def project(i, s, n, warm_up=0):
             if not ok(i):
                 return
             xc, xsc = live[("xc", i, s)]
             s1 = psum.tile([P, 512], F32, name="s1", tag="s1", bufs=4)
+            for step in range(warm_up):
+                nc.tensor.matmul(s1[:], lhsT=zeros[:, 0:P], rhs=zeros[:], start=True, stop=True)
             for c in range(4):
                 nc.tensor.matmul_mx(
                     out=s1[:, c * P : (c + 1) * P],
@@ -313,7 +316,7 @@ def tile_attentionmm_pa_t_kernel(tc, x1, x2, W1, W2, b1, b2, out):
             pb = psum.tile([P, 512], F32, name="pb", tag="s1", bufs=4)
             nc.tensor.matmul(pb[:], lhsT=ident[:], rhs=live[("a_sb", i)][:], start=True, stop=False)
             nc.tensor.matmul(
-                pb[:], lhsT=ident_bf[:], rhs=live["bias_plain"][:, 512:1024], start=False, stop=True
+                pb[:], lhsT=ident_bf[:], rhs=live["bias_plain"][:], start=False, stop=True
             )
             live[("pb", i)] = pb
 
@@ -332,13 +335,7 @@ def tile_attentionmm_pa_t_kernel(tc, x1, x2, W1, W2, b1, b2, out):
                 add_bias(i, 0, n)
                 if n == 0:
                     relu_pool(i, 0, 0, 512)
-                if i > 0:
-                    project(i, 1, n)
-            if i == 0:
-                quantise_w(1)
-                quantise_x(0, 1)
-                for n in range(4):
-                    project(0, 1, n)
+                project(i, 1, n)
             relu_act(i, 0, 1024, 2048)
             relu_vec(i, 0, 512, 1024)
             if i < N_UNITS - 1:
@@ -370,70 +367,123 @@ def tile_attentionmm_pa_t_kernel(tc, x1, x2, W1, W2, b1, b2, out):
             normalise(i - 2, 0, 3)
             max_and_exp(i - 1)
 
+        def scale_act(i, q):
+            ex = live[("ex", i)]
+            nc.scalar.activation(
+                out=ex[:, q * T : (q + 1) * T],
+                in_=ex[:, q * T : (q + 1) * T],
+                func=ACT.Copy,
+                scale=live[("recip", i)][:, q : q + 1],
+            )
+
         def tail(i):
             half = 2 * UNIT
-            normalise(i - 3, 3, 4)
+            reciprocals(i - 3, 3, 4)
+            scale_act(i - 3, 3)
             store(i - 3, 0, 4)
             add_bias(i, 1, 0)
             add_bias(i, 1, 1)
-            normalise(i - 2, 0, 4)
-            store(i - 2, 0, 4)
-            max_and_exp(i - 1)
+            row_max(i - 1, 0, 0, 2)
+            exps(i - 1, 0, 0)
+            exps(i - 1, 0, 1)
             relu_vec(i, 1, 0, half)
             quantise_e(i, 0, 0, 4 * UNIT)
-            add_bias(i, 1, 2)
             quantise_e(i, 1, 0, half)
+            row_max(i - 1, 1, 0, 2)
+            exps(i - 1, 1, 0)
+            exps(i - 1, 1, 1)
             scores(i, 0)
+            add_bias(i, 1, 2)
             add_bias(i, 1, 3)
-            normalise(i - 1, 0, 4)
-            store(i - 1, 0, 4)
-            relu_vec(i, 1, half, 2 * half)
+            reciprocals(i - 2, 0, 4)
+            for q in range(4):
+                scale_act(i - 2, q)
+            store(i - 2, 0, 4)
             row_max(i, 0, 0, 2)
             exps(i, 0, 0)
             exps(i, 0, 1)
+            relu_vec(i, 1, half, 2 * half)
+            reciprocals(i - 1, 0, 4)
             quantise_e(i, 1, half, 2 * half)
             scores(i, 1)
-            row_max(i, 1, 0, 1)
+            for q in range(4):
+                scale_vec(i - 1, q)
+            store(i - 1, 0, 4)
+            row_max(i, 1, 0, 2)
             exps(i, 1, 0)
-            row_max(i, 1, 1, 2)
             exps(i, 1, 1)
-            for bb in range(2):
-                reciprocals(i, 2 * bb, 2 * bb + 2)
-                scale_vec(i, 2 * bb)
-                scale_vec(i, 2 * bb + 1)
-                store(i, 2 * bb, 2 * bb + 2)
+            reciprocals(i, 0, 2)
+            scale_vec(i, 0)
+            scale_vec(i, 1)
+            store(i, 0, 2)
+            reciprocals(i, 2, 4)
+            scale_vec(i, 2)
+            scale_act(i, 3)
+            store(i, 2, 4)
 
         ident = const.tile([P, P], F32, name="ident")
         make_identity(nc, ident[:])
         ident_bf = const.tile([P, P], BF16, name="ident_bf")
         make_identity(nc, ident_bf[:])
+        load_x(0, 0, 0, 2)
         load_w(0)
-        load_x(0, 0)
-        load_w(1)
+        load_x(0, 0, 2, 4)
         load_b(0)
+        load_w(1)
         load_x(0, 1)
         load_b(1)
         for i in range(1, LOAD_AHEAD):
             load_x(i, 0)
             load_x(i, 1)
 
-        regroup_w(0, True)
-        regroup_w(1, False)
-        transpose_x(0, 0)
-        drain_x(0, 0)
+        zeros = const.tile([P, 512], BF16, name="zeros")
+        nc.vector.memset(zeros[:], 0.0)
+        warm = psum.tile([P, 512], F32, name="warm", tag="sc")
+        for step in range(5):
+            nc.tensor.matmul(warm[:], lhsT=zeros[:, 0:P], rhs=zeros[:], start=True, stop=True)
+        regroup_w(0)
+        transpose_x(0, 0, (0,))
+        drain_x(0, 0, (0,))
         quantise_w(0)
+        transpose_x(0, 0, (1,))
+        drain_x(0, 0, (1,))
         transpose_b(0)
-        drain_b(0)
-        quantise_x(0, 0)
-        for n in range(4):
-            project(0, 0, n)
+        drain_b(0, 0)
+        drain_b(0, 1)
+        quantise_x(0, 0, 0, 1024)
+        project(0, 0, 0)
+        project(0, 0, 1, 1)
+        quantise_x(0, 0, 1024, 2048)
+        project(0, 0, 2)
+        project(0, 0, 3, 1)
+        regroup_w(1)
         transpose_x(0, 1)
         drain_x(0, 1)
+        add_bias(0, 0, 0)
+        add_bias(0, 0, 1)
         transpose_b(1)
-        drain_b(1)
+        drain_b(1, 0)
+        drain_b(1, 1)
         transpose_x(1, 0)
+        quantise_w(1)
+        quantise_x(0, 1)
+        drain_x(1, 0)
+        project(0, 1, 3)
+        project(0, 1, 0)
+        add_bias(0, 0, 2)
+        project(0, 1, 1)
+        add_bias(0, 0, 3)
+        project(0, 1, 2)
+        relu_act(0, 0, 1024, 2048)
+        relu_vec(0, 0, 0, 1024)
+        detour_out(0)
+        transpose_x(1, 1)
+        quantise_x(1, 0)
+        load_x(LOAD_AHEAD, 0)
+        load_x(LOAD_AHEAD, 1)
+        second_half(0)
 
-        for i in range(N_UNITS - 1):
+        for i in range(1, N_UNITS - 1):
             first_half(i)
             second_half(i)
         first_half(N_UNITS - 1)

@@ -84,26 +84,30 @@ def tile_attentionmm_pa_t_kernel(tc, x1, x2, W1, W2, b1, b2, out):
 
         def transpose_b(s):
             bias_t.append(const.tile([P, T * 4], BF16, name="bias_t%d" % s))
+            b_f32 = b_raw[s][:].bitcast(F32)
+            bt = psum.tile([P, 512], F32, name="bt", tag="sc")
             for h in range(2):
-                bt = psum.tile([P, 4 * P], BF16, name="bt", tag="sc")
-                for c in range(4):
+                for u in range(2):
                     nc.tensor.transpose(
-                        bt[:, c * P : (c + 1) * P],
-                        b_raw[s][:, h * E + c : (h + 1) * E : 4],
-                        ident_bf[:],
+                        bt[:, (2 * h + u) * P : (2 * h + u + 1) * P],
+                        b_f32[:, h * 256 + u : (h + 1) * 256 : 2],
+                        ident[:],
                     )
-                live[("bt", s, h)] = bt
+            live[("bt", s)] = bt
 
-        def drain_b(s, h):
-            bt = live[("bt", s, h)]
+        def drain_b(s):
             nc.scalar.copy(
-                out=bias_t[s][:, h * 512 : (h + 1) * 512].rearrange("p (t c) -> p t c", c=4),
-                in_=bt[:].rearrange("p (c t) -> p t c", c=4),
+                out=bias_t[s][:].bitcast(F32).rearrange("p (h t u) -> p h t u", h=2, u=2),
+                in_=live[("bt", s)][:].rearrange("p (h u t) -> p h t u", h=2, u=2),
             )
-            if s == 1 and h == 1:
-                plain = const.tile([P, 4 * P], BF16, name="bias_plain")
-                nc.scalar.copy(out=plain[:], in_=bt[:])
-                live["bias_plain"] = plain
+
+        def plain_b():
+            plain = const.tile([P, 4 * P], BF16, name="bias_plain")
+            nc.scalar.copy(
+                out=plain[:].rearrange("p (c t) -> p c t", c=4),
+                in_=bias_t[1][:, 512:1024].rearrange("p (t c) -> p c t", c=4),
+            )
+            live["bias_plain"] = plain
 
         def transpose_x(i, s, halves=(0, 1)):
             if not ok(i):
@@ -336,8 +340,8 @@ def tile_attentionmm_pa_t_kernel(tc, x1, x2, W1, W2, b1, b2, out):
                 if n == 0:
                     relu_pool(i, 0, 0, 512)
                 project(i, 1, n)
+            relu_act(i, 0, 512, 1024)
             relu_act(i, 0, 1024, 2048)
-            relu_vec(i, 0, 512, 1024)
             if i < N_UNITS - 1:
                 detour_out(i)
             transpose_x(i + 1, 1)
@@ -348,8 +352,6 @@ def tile_attentionmm_pa_t_kernel(tc, x1, x2, W1, W2, b1, b2, out):
 
         def second_half(i):
             drain_x(i + 1, 1)
-            normalise(i - 3, 3, 4)
-            store(i - 3, 0, 4)
             add_bias(i, 1, 0)
             relu_pool(i, 1, 0, 512)
             detour_add(i)
@@ -364,7 +366,8 @@ def tile_attentionmm_pa_t_kernel(tc, x1, x2, W1, W2, b1, b2, out):
             transpose_x(i + 2, 0)
             quantise_e(i, 0, 0, 4 * UNIT)
             quantise_x(i + 1, 1)
-            normalise(i - 2, 0, 3)
+            normalise(i - 2, 0, 4)
+            store(i - 2, 0, 4)
             max_and_exp(i - 1)
 
         def scale_act(i, q):
@@ -378,9 +381,6 @@ def tile_attentionmm_pa_t_kernel(tc, x1, x2, W1, W2, b1, b2, out):
 
         def tail(i):
             half = 2 * UNIT
-            reciprocals(i - 3, 3, 4)
-            scale_act(i - 3, 3)
-            store(i - 3, 0, 4)
             add_bias(i, 1, 0)
             add_bias(i, 1, 1)
             row_max(i - 1, 0, 0, 2)
@@ -439,31 +439,33 @@ def tile_attentionmm_pa_t_kernel(tc, x1, x2, W1, W2, b1, b2, out):
         zeros = const.tile([P, 512], BF16, name="zeros")
         nc.vector.memset(zeros[:], 0.0)
         warm = psum.tile([P, 512], F32, name="warm", tag="sc")
-        for step in range(5):
+        for step in range(6):
             nc.tensor.matmul(warm[:], lhsT=zeros[:, 0:P], rhs=zeros[:], start=True, stop=True)
         regroup_w(0)
         transpose_x(0, 0, (0,))
         drain_x(0, 0, (0,))
         quantise_w(0)
+        for step in range(2):
+            nc.tensor.matmul(warm[:], lhsT=zeros[:, 0:P], rhs=zeros[:], start=True, stop=True)
         transpose_x(0, 0, (1,))
         drain_x(0, 0, (1,))
+        for step in range(2):
+            nc.tensor.matmul(warm[:], lhsT=zeros[:, 0:P], rhs=zeros[:], start=True, stop=True)
         transpose_b(0)
-        drain_b(0, 0)
-        drain_b(0, 1)
+        drain_b(0)
         quantise_x(0, 0, 0, 1024)
         project(0, 0, 0)
-        project(0, 0, 1, 1)
+        project(0, 0, 1)
         quantise_x(0, 0, 1024, 2048)
         project(0, 0, 2)
-        project(0, 0, 3, 1)
+        project(0, 0, 3)
         regroup_w(1)
         transpose_x(0, 1)
         drain_x(0, 1)
         add_bias(0, 0, 0)
         add_bias(0, 0, 1)
         transpose_b(1)
-        drain_b(1, 0)
-        drain_b(1, 1)
+        drain_b(1)
         transpose_x(1, 0)
         quantise_w(1)
         quantise_x(0, 1)
@@ -481,6 +483,7 @@ def tile_attentionmm_pa_t_kernel(tc, x1, x2, W1, W2, b1, b2, out):
         quantise_x(1, 0)
         load_x(LOAD_AHEAD, 0)
         load_x(LOAD_AHEAD, 1)
+        plain_b()
         second_half(0)
 
         for i in range(1, N_UNITS - 1):

@@ -181,8 +181,8 @@ def tile_attentionmm_pa_t_kernel(tc, x1, x2, W1, W2, b1, b2, out):
             t0 = (n % 2) * P
             nc.vector.tensor_tensor(
                 out=eg[:, n * 512 : (n + 1) * 512].rearrange("p (t c) -> p t c", c=4),
-                in0=live[("s1", i, s, n)][:].rearrange("p (c t) -> p t c", c=4),
-                in1=bias_t[s][:, t0 * 4 : (t0 + P) * 4].rearrange("p (t c) -> p t c", c=4),
+                in0=bias_t[s][:, t0 * 4 : (t0 + P) * 4].rearrange("p (t c) -> p t c", c=4),
+                in1=live[("s1", i, s, n)][:].rearrange("p (c t) -> p t c", c=4),
                 op=ALU.add,
             )
 

@@ -340,8 +340,11 @@ def tile_attentionmm_pa_t_kernel(tc, x1, x2, W1, W2, b1, b2, out):
                 if n == 0:
                     relu_pool(i, 0, 0, 512)
                 project(i, 1, n)
-            relu_act(i, 0, 512, 1024)
+            if i % 2 == 0:
+                relu_act(i, 0, 512, 1024)
             relu_act(i, 0, 1024, 2048)
+            if i % 2 == 1:
+                relu_vec(i, 0, 512, 1024)
             if i < N_UNITS - 1:
                 detour_out(i)
             transpose_x(i + 1, 1)

from contextlib import ExitStack

import concourse.mybir as mybir
from concourse.masks import make_identity

FLOPS = 2 * (2 * 8192 * 512 * 512) + 2 * 32 * 256 * 256 * 512

BF16 = mybir.dt.bfloat16
F32 = mybir.dt.float32
U32 = mybir.dt.uint32
U8 = mybir.dt.uint8
FP8X4 = mybir.dt.float8_e4m3fn_x4
ALU = mybir.AluOpType
ACT = mybir.ActivationFunctionType

P = 128
B, T, E = 32, 256, 512
UNIT = 512
N_UNITS = B * T // UNIT
LOAD_AHEAD = 6
BIG = 3.4028234e38


def tile_attentionmm_pa_t_kernel(tc, x1, x2, W1, W2, b1, b2, out):
    nc = tc.nc
    xs_dram = [x1.rearrange("b t k -> (b t) k"), x2.rearrange("b t k -> (b t) k")]
    ws_dram = [W1, W2]
    bs_dram = [b1, b2]
    out_view = out.rearrange("b (c p) j -> p (b c) j", p=P)

    with ExitStack() as ctx:
        ctx.enter_context(tc.manual_schedule())
        const = ctx.enter_context(tc.tile_pool(name="const", bufs=1))
        xin = ctx.enter_context(tc.tile_pool(name="xin", bufs=2 * LOAD_AHEAD))
        work = ctx.enter_context(tc.tile_pool(name="work", bufs=3))
        small = ctx.enter_context(tc.tile_pool(name="small", bufs=4))
        psum = ctx.enter_context(tc.psum_pool(name="psum", bufs=2))

        live = {}
        w_raw, b_raw, w_grp, w_codes, w_scales, bias_t = [], [], [], [], [], []

        def ok(i):
            return 0 <= i < N_UNITS

        def load_x(i, s, n0=0, n1=4):
            if not ok(i):
                return
            if n0 == 0:
                live[("x", i, s)] = xin.tile([P, 4 * E], BF16, name="x_sb", tag="x_sb")
            nc.sync.dma_start(
                out=live[("x", i, s)][:, n0 * E : n1 * E].rearrange("p (n k) -> p n k", n=n1 - n0),
                in_=xs_dram[s][i * UNIT + n0 * P : i * UNIT + n1 * P, :].rearrange("(n p) k -> p n k", p=P),
            )

        def load_w(s):
            wr = const.tile([P, 4 * E], BF16, name="w_raw%d" % s)
            nc.sync.dma_start(
                out=wr[:],
                in_=ws_dram[s].rearrange("(p j) f -> p (j f)", j=4),
            )
            w_raw.append(wr)

        def load_b(s):
            br = const.tile([P, 2 * E], BF16, name="b_raw%d" % s)
            nc.sync.dma_start(
                out=br[:].rearrange("p (h f) -> p h f", h=2),
                in_=bs_dram[s].rearrange("(h p) f -> p h f", p=P),
            )
            b_raw.append(br)

        def regroup_w(s):
            wg = const.tile([P, 4 * E], BF16, name="w_grp%d" % s, align_bytes=64)
            dst = wg[:].rearrange("p (c m j) -> p c m j", c=4, j=4)
            src = w_raw[s][:].rearrange("p (j m c) -> p c m j", j=4, c=4)
            nc.vector.tensor_copy(out=dst, in_=src)
            w_grp.append(wg)

        def quantise_w(s):
            wc = const.tile([P, E], U32, name="w_codes%d" % s, align_bytes=64)
            wsc = const.tile([P, E], U8, name="w_scales%d" % s, align_bytes=64)
            nc.vector.quantize_mx(out=wc[:].bitcast(FP8X4), scales=wsc[:], in_=w_grp[s][:])
            w_codes.append(wc)
            w_scales.append(wsc)

        def transpose_b(s):
            bias_t.append(const.tile([P, T * 4], BF16, name="bias_t%d" % s))
            b_f32 = b_raw[s][:].bitcast(F32)
            bt = psum.tile([P, 512], F32, name="bt", tag="sc")
            for h in range(2):
                for u in range(2):
                    nc.tensor.transpose(
                        bt[:, (2 * h + u) * P : (2 * h + u + 1) * P],
                        b_f32[:, h * 256 + u : (h + 1) * 256 : 2],
                        ident[:],
                    )
            live[("bt", s)] = bt

        def drain_b(s):
            nc.scalar.copy(
                out=bias_t[s][:].bitcast(F32).rearrange("p (h t u) -> p h t u", h=2, u=2),
                in_=live[("bt", s)][:].rearrange("p (h u t) -> p h t u", h=2, u=2),
            )

        def plain_b():
            plain = const.tile([P, 4 * P], BF16, name="bias_plain")
            nc.scalar.copy(
                out=plain[:].rearrange("p (c t) -> p c t", c=4),
                in_=bias_t[1][:, 512:1024].rearrange("p (t c) -> p c t", c=4),
            )
            live["bias_plain"] = plain

        def transpose_x(i, s, halves=(0, 1)):
            if not ok(i):
                return
            x_f32 = live[("x", i, s)][:].bitcast(F32)
            for h in halves:
                xt = psum.tile([P, 512], F32, name="xt", tag="xt")
                for nn in range(2):
                    for u in range(2):
                        n = 2 * h + nn
                        nc.tensor.transpose(
                            xt[:, u * 256 + nn * P : u * 256 + (nn + 1) * P],
                            x_f32[:, n * 256 + u : (n + 1) * 256 : 2],
                            ident[:],
                        )
                live[("xt", i, s, h)] = xt

        def drain_x(i, s, halves=(0, 1)):
            if not ok(i):
                return
            if halves[0] == 0:
                live[("xg", i, s)] = work.tile([P, 4 * UNIT], BF16, name="xg", tag="xg", align_bytes=64)
            xg_f32 = live[("xg", i, s)][:].bitcast(F32)
            for h in halves:
                nc.scalar.copy(
                    out=xg_f32[:, h * 512 : (h + 1) * 512].rearrange("p (t u) -> p t u", u=2),
                    in_=live[("xt", i, s, h)][:].rearrange("p (u t) -> p t u", u=2),
                )

        def quantise_x(i, s, lo=0, hi=4 * UNIT):
            if not ok(i):
                return
            if lo == 0:
                xc = work.tile([P, UNIT], U32, name="xc", tag="xc", align_bytes=64)
                xsc = work.tile([P, UNIT], U8, name="xsc", tag="xsc", align_bytes=64)
                live[("xc", i, s)] = (xc, xsc)
            xc, xsc = live[("xc", i, s)]
            nc.vector.quantize_mx(
                out=xc[:, lo // 4 : hi // 4].bitcast(FP8X4),
                scales=xsc[:, lo // 4 : hi // 4],
                in_=live[("xg", i, s)][:, lo:hi],
            )

        def project(i, s, n, warm_up=0):
            if not ok(i):
                return
            xc, xsc = live[("xc", i, s)]
            s1 = psum.tile([P, 512], F32, name="s1", tag="s1", bufs=4)
            for step in range(warm_up):
                nc.tensor.matmul(s1[:], lhsT=zeros[:, 0:P], rhs=zeros[:], start=True, stop=True)
            for c in range(4):
                nc.tensor.matmul_mx(
                    out=s1[:, c * P : (c + 1) * P],
                    lhsT=w_codes[s][:, c * P : (c + 1) * P].bitcast(FP8X4),
                    lhsT_scale=w_scales[s][:, c * P : (c + 1) * P],
                    rhs=xc[:, n * P : (n + 1) * P].bitcast(FP8X4),
                    rhs_scale=xsc[:, n * P : (n + 1) * P],
                    start=True,
                    stop=True,
                )
            live[("s1", i, s, n)] = s1

        def add_bias(i, s, n):
            if not ok(i):
                return
            if n == 0:
                live[("eg", i, s)] = work.tile(
                    [P, 4 * UNIT], BF16, name="eg", tag="eg", align_bytes=64
                )
            eg = live[("eg", i, s)]
            t0 = (n % 2) * P
            nc.vector.tensor_tensor(
                out=eg[:, n * 512 : (n + 1) * 512].rearrange("p (t c) -> p t c", c=4),
                in0=bias_t[s][:, t0 * 4 : (t0 + P) * 4].rearrange("p (t c) -> p t c", c=4),
                in1=live[("s1", i, s, n)][:].rearrange("p (c t) -> p t c", c=4),
                op=ALU.add,
            )

        def relu_pool(i, s, lo, hi):
            if not ok(i):
                return
            eg = live[("eg", i, s)]
            nc.gpsimd.tensor_scalar(
                out=eg[:, lo:hi], in0=eg[:, lo:hi], scalar1=BIG, scalar2=0.0, op0=ALU.min, op1=ALU.max
            )

        def relu_act(i, s, lo, hi):
            if not ok(i):
                return
            eg = live[("eg", i, s)]
            nc.scalar.activation(out=eg[:, lo:hi], in_=eg[:, lo:hi], func=ACT.Relu)

        def relu_vec(i, s, lo, hi):
            eg = live[("eg", i, s)]
            nc.vector.tensor_scalar_max(out=eg[:, lo:hi], in0=eg[:, lo:hi], scalar1=0.0)

        def quantise_e(i, s, lo, hi):
            if not ok(i):
                return
            if lo == 0:
                ec = work.tile([P, UNIT], U32, name="ec", tag="ec", bufs=4, align_bytes=64)
                esc = work.tile([P, UNIT], U8, name="esc", tag="esc", bufs=4, align_bytes=64)
                live[("ec", i, s)] = (ec, esc)
            ec, esc = live[("ec", i, s)]
            nc.vector.quantize_mx(
                out=ec[:, lo // 4 : hi // 4].bitcast(FP8X4),
                scales=esc[:, lo // 4 : hi // 4],
                in_=live[("eg", i, s)][:, lo:hi],
            )

        def scores(i, bb):
            if not ok(i):
                return
            e1c, e1s = live[("ec", i, 0)]
            e2c, e2s = live[("ec", i, 1)]
            sc = psum.tile([P, 512], F32, name="sc", tag="sc")
            for c in range(2):
                nc.tensor.matmul_mx(
                    out=sc[:, c * T : (c + 1) * T],
                    lhsT=e2c[:, bb * T + c * P : bb * T + (c + 1) * P].bitcast(FP8X4),
                    lhsT_scale=e2s[:, bb * T + c * P : bb * T + (c + 1) * P],
                    rhs=e1c[:, bb * T : (bb + 1) * T].bitcast(FP8X4),
                    rhs_scale=e1s[:, bb * T : (bb + 1) * T],
                    start=True,
                    stop=True,
                )
            live[("sc", i, bb)] = sc

        def row_max(i, bb, c0, c1):
            if not ok(i):
                return
            if bb == 0 and c0 == 0:
                live[("neg_max", i)] = small.tile([P, 4], F32, name="neg_max", tag="neg_max")
                live[("sums", i)] = small.tile([P, 4], F32, name="sums", tag="sums")
                live[("ex", i)] = work.tile([P, 4 * T], F32, name="ex", tag="ex", bufs=4)
            nc.vector.tensor_reduce(
                out=live[("neg_max", i)][:, 2 * bb + c0 : 2 * bb + c1],
                in_=live[("sc", i, bb)][:, c0 * T : c1 * T].rearrange("p (c j) -> p c j", j=T),
                axis=mybir.AxisListType.X,
                op=ALU.max,
                negate=True,
            )

        def exps(i, bb, c):
            if not ok(i):
                return
            q = 2 * bb + c
            nc.scalar.activation(
                out=live[("ex", i)][:, q * T : (q + 1) * T],
                in_=live[("sc", i, bb)][:, c * T : (c + 1) * T],
                func=ACT.Exp,
                bias=live[("neg_max", i)][:, q : q + 1],
                scale=1.0,
                accum_out=live[("sums", i)][:, q : q + 1],
            )

        def reciprocals(i, q0, q1):
            if not ok(i):
                return
            if q0 == 0:
                live[("recip", i)] = small.tile([P, 4], F32, name="recip", tag="recip")
            nc.vector.reciprocal(out=live[("recip", i)][:, q0:q1], in_=live[("sums", i)][:, q0:q1])

        def scale_pool(i, q):
            if not ok(i):
                return
            ex = live[("ex", i)]
            nc.gpsimd.tensor_scalar(
                out=ex[:, q * T : (q + 1) * T],
                in0=ex[:, q * T : (q + 1) * T],
                scalar1=live[("recip", i)][:, q : q + 1],
                scalar2=0.0,
                op0=ALU.mult,
                op1=ALU.add,
            )

        def scale_vec(i, q):
            ex = live[("ex", i)]
            nc.vector.tensor_scalar_mul(
                out=ex[:, q * T : (q + 1) * T],
                in0=ex[:, q * T : (q + 1) * T],
                scalar1=live[("recip", i)][:, q : q + 1],
            )

        def store(i, q0, q1):
            if not ok(i):
                return
            nc.sync.dma_start(
                out=out_view[:, 4 * i + q0 : 4 * i + q1, :],
                in_=live[("ex", i)][:, q0 * T : q1 * T].rearrange("p (q j) -> p q j", j=T),
            )

        def max_and_exp(i):
            for bb in range(2):
                row_max(i, bb, 0, 2)
                exps(i, bb, 0)
                exps(i, bb, 1)

        def normalise(i, q0, q1):
            reciprocals(i, q0, q1)
            for q in range(q0, q1):
                scale_pool(i, q)

        def detour_out(i):
            a_sb = work.tile([P, 512], F32, name="a_sb", tag="a_sb")
            nc.scalar.copy(out=a_sb[:], in_=live[("s1", i, 1, 3)][:])
            live[("a_sb", i)] = a_sb

        def detour_add(i):
            pb = psum.tile([P, 512], F32, name="pb", tag="s1", bufs=4)
            nc.tensor.matmul(pb[:], lhsT=ident[:], rhs=live[("a_sb", i)][:], start=True, stop=False)
            nc.tensor.matmul(
                pb[:], lhsT=ident_bf[:], rhs=live["bias_plain"][:], start=False, stop=True
            )
            live[("pb", i)] = pb

        def detour_relu(i):
            nc.scalar.activation(
                out=live[("eg", i, 1)][:, 1536:2048].rearrange("p (t c) -> p t c", c=4),
                in_=live[("pb", i)][:].rearrange("p (c t) -> p t c", c=4),
                func=ACT.Relu,
            )

        def first_half(i):
            load_x(i + LOAD_AHEAD, 0)
            load_x(i + LOAD_AHEAD, 1)
            drain_x(i + 1, 0)
            for n in range(4):
                add_bias(i, 0, n)
                if n == 0:
                    relu_pool(i, 0, 0, 512)
                project(i, 1, n)
            if i % 2 == 0:
                relu_act(i, 0, 512, 1024)
            relu_act(i, 0, 1024, 2048)
            if i % 2 == 1:
                relu_vec(i, 0, 512, 1024)
            if i < N_UNITS - 1:
                detour_out(i)
            transpose_x(i + 1, 1)
            quantise_e(i - 1, 1, 0, 4 * UNIT)
            scores(i - 1, 0)
            scores(i - 1, 1)
            quantise_x(i + 1, 0)

        def second_half(i):
            drain_x(i + 1, 1)
            add_bias(i, 1, 0)
            relu_pool(i, 1, 0, 512)
            detour_add(i)
            add_bias(i, 1, 1)
            project(i + 1, 0, 0)
            add_bias(i, 1, 2)
            project(i + 1, 0, 1)
            project(i + 1, 0, 2)
            relu_act(i, 1, 512, 1536)
            detour_relu(i)
            project(i + 1, 0, 3)
            transpose_x(i + 2, 0)
            quantise_e(i, 0, 0, 4 * UNIT)
            quantise_x(i + 1, 1)
            normalise(i - 2, 0, 4)
            store(i - 2, 0, 4)
            max_and_exp(i - 1)

        def scale_act(i, q):
            ex = live[("ex", i)]
            nc.scalar.activation(
                out=ex[:, q * T : (q + 1) * T],
                in_=ex[:, q * T : (q + 1) * T],
                func=ACT.Copy,
                scale=live[("recip", i)][:, q : q + 1],
            )

        def tail(i):
            half = 2 * UNIT
            add_bias(i, 1, 0)
            add_bias(i, 1, 1)
            row_max(i - 1, 0, 0, 2)
            exps(i - 1, 0, 0)
            exps(i - 1, 0, 1)
            relu_vec(i, 1, 0, half)
            quantise_e(i, 0, 0, 4 * UNIT)
            quantise_e(i, 1, 0, half)
            row_max(i - 1, 1, 0, 2)
            exps(i - 1, 1, 0)
            exps(i - 1, 1, 1)
            scores(i, 0)
            add_bias(i, 1, 2)
            add_bias(i, 1, 3)
            reciprocals(i - 2, 0, 4)
            for q in range(4):
                scale_act(i - 2, q)
            store(i - 2, 0, 4)
            row_max(i, 0, 0, 2)
            exps(i, 0, 0)
            exps(i, 0, 1)
            relu_vec(i, 1, half, 2 * half)
            reciprocals(i - 1, 0, 4)
            quantise_e(i, 1, half, 2 * half)
            scores(i, 1)
            for q in range(4):
                scale_vec(i - 1, q)
            store(i - 1, 0, 4)
            row_max(i, 1, 0, 2)
            exps(i, 1, 0)
            exps(i, 1, 1)
            reciprocals(i, 0, 2)
            scale_vec(i, 0)
            scale_vec(i, 1)
            store(i, 0, 2)
            reciprocals(i, 2, 4)
            scale_vec(i, 2)
            scale_act(i, 3)
            store(i, 2, 4)

        ident = const.tile([P, P], F32, name="ident")
        make_identity(nc, ident[:])
        ident_bf = const.tile([P, P], BF16, name="ident_bf")
        make_identity(nc, ident_bf[:])
        load_x(0, 0, 0, 2)
        load_w(0)
        load_x(0, 0, 2, 4)
        load_b(0)
        load_w(1)
        load_x(0, 1)
        load_b(1)
        for i in range(1, LOAD_AHEAD):
            load_x(i, 0)
            load_x(i, 1)

        zeros = const.tile([P, 512], BF16, name="zeros")
        nc.vector.memset(zeros[:], 0.0)
        warm = psum.tile([P, 512], F32, name="warm", tag="sc")
        for step in range(6):
            nc.tensor.matmul(warm[:], lhsT=zeros[:, 0:P], rhs=zeros[:], start=True, stop=True)
        regroup_w(0)
        transpose_x(0, 0, (0,))
        drain_x(0, 0, (0,))
        quantise_w(0)
        for step in range(2):
            nc.tensor.matmul(warm[:], lhsT=zeros[:, 0:P], rhs=zeros[:], start=True, stop=True)
        transpose_x(0, 0, (1,))
        drain_x(0, 0, (1,))
        for step in range(2):
            nc.tensor.matmul(warm[:], lhsT=zeros[:, 0:P], rhs=zeros[:], start=True, stop=True)
        transpose_b(0)
        drain_b(0)
        quantise_x(0, 0, 0, 1024)
        project(0, 0, 0)
        project(0, 0, 1)
        quantise_x(0, 0, 1024, 2048)
        project(0, 0, 2)
        project(0, 0, 3)
        regroup_w(1)
        transpose_x(0, 1)
        drain_x(0, 1)
        add_bias(0, 0, 0)
        add_bias(0, 0, 1)
        transpose_b(1)
        drain_b(1)
        transpose_x(1, 0)
        quantise_w(1)
        quantise_x(0, 1)
        drain_x(1, 0)
        project(0, 1, 3)
        project(0, 1, 0)
        add_bias(0, 0, 2)
        project(0, 1, 1)
        add_bias(0, 0, 3)
        project(0, 1, 2)
        relu_act(0, 0, 1024, 2048)
        relu_vec(0, 0, 0, 1024)
        detour_out(0)
        transpose_x(1, 1)
        quantise_x(1, 0)
        load_x(LOAD_AHEAD, 0)
        load_x(LOAD_AHEAD, 1)
        plain_b()
        second_half(0)

        for i in range(1, N_UNITS - 1):
            first_half(i)
            second_half(i)
        first_half(N_UNITS - 1)
        tail(N_UNITS - 1)
